import numpy as np
import ml_dtypes


BF16 = ml_dtypes.bfloat16


def bf(x):
    return np.asarray(x, np.float32).astype(BF16)


def f64(x):
    return np.asarray(x).astype(np.float64)


E2M1 = np.array([0.0, 0.5, 1.0, 1.5, 2.0, 3.0, 4.0, 6.0, -0.0, -0.5, -1.0, -1.5, -2.0, -3.0, -4.0, -6.0])


def pack_weight(w, fmt):
    k, n = w.shape
    w = f64(bf(w)).reshape(k // 32, 32, n)
    amax = np.abs(w).max(1)
    if fmt == "e4m3":
        byte = np.frexp(amax)[1] - 1 + 127 - 7
    else:
        mant, ex = np.frexp(amax / 6.0)
        byte = np.where(mant > 0.5, ex, ex - 1) + 127
    byte = np.clip(np.where(amax > 0, byte, 1), 1, 254)
    scaled = (w * np.exp2(127.0 - byte)[:, None, :]).reshape(k, n).astype(np.float32)
    by_word = np.ascontiguousarray(scaled.reshape(k // 512, 128, 4, n).transpose(0, 1, 3, 2))
    if fmt == "e4m3":
        words = by_word.astype(ml_dtypes.float8_e4m3fn).view(np.uint8)
    else:
        c = by_word.astype(ml_dtypes.float4_e2m1fn).view(np.uint8) & 0xF
        words = c[..., 0::2] | (c[..., 1::2] << 4)
    return np.ascontiguousarray(words), np.ascontiguousarray(byte.astype(np.uint8).reshape(k // 512, 16, n))


def unpack_weight(words, scales, fmt):
    g, p, n, _ = words.shape
    if fmt == "e4m3":
        vals = np.ascontiguousarray(words).view(ml_dtypes.float8_e4m3fn).astype(np.float64)
    else:
        nib = np.empty((g, p, n, 4), np.uint8)
        nib[..., 0::2] = words & 0xF
        nib[..., 1::2] = words >> 4
        vals = E2M1[nib]
    vals = vals * np.repeat(np.exp2(scales.astype(np.float64) - 127.0), 8, axis=1)[..., None]
    return vals.transpose(0, 1, 3, 2).reshape(g * 512, n)

def pack4(w):
    words, scales = pack_weight(w, "e2m1")
    return words.reshape(words.shape[0], 128, -1), scales


def unpack4(words, scales):
    return unpack_weight(words.reshape(words.shape[0], 128, -1, 2), scales, "e2m1")


def kspread(k):
    return np.exp2(np.repeat(np.random.randint(-6, 7, k // 32), 32).astype(np.float64))


B, L, E, H = 2, 64, 3584, 16
HD = E // H
EPS = 1e-12


def l2_normalize(t):
    n = np.sqrt(np.sum(t * t, axis=-1, keepdims=True))
    return t / np.maximum(n, EPS)


def setup_inputs():
    s = kspread(E)
    x = np.random.standard_normal((B, L, E)) * s
    x_words, x_scales = pack4(np.ascontiguousarray(x.reshape(B * L, E).T))
    w = np.random.standard_normal((3 * E, E)) / np.sqrt(E) / s[None, :]
    words, scales = pack4(np.ascontiguousarray(w.T))
    b = bf(np.random.standard_normal(3 * E) * 0.3)
    return {"x_words": x_words, "x_scales": x_scales, "W_words": words, "W_scales": scales, "b": b}


def reference(x_words, x_scales, W_words, W_scales, b):
    x = unpack4(x_words, x_scales).T.reshape(B, L, E)
    y = (x @ unpack4(W_words, W_scales)) + f64(b)
    y = y.reshape(B, L, H, 3, HD)
    q = np.transpose(y[..., 0, :], (0, 2, 1, 3))
    k = np.transpose(y[..., 1, :], (0, 2, 1, 3))
    v = np.transpose(y[..., 2, :], (0, 2, 1, 3))
    return l2_normalize(q), l2_normalize(k), v

@@ -1,0 +1,248 @@
+from contextlib import ExitStack
+
+import concourse.mybir as mybir
+from concourse.masks import make_identity
+
+F32 = mybir.dt.float32
+BF16 = mybir.dt.bfloat16
+U8 = mybir.dt.uint8
+I32 = mybir.dt.int32
+FP4X4 = mybir.dt.float4_e2m1fn_x4
+ALU = mybir.AluOpType
+ACT = mybir.ActivationFunctionType
+
+P = 128
+B, L, E, H = 2, 64, 3584, 16
+HD = E // H
+HEAD_COLS = 3 * HD
+COLS = 3 * E
+PASSES = E // 512
+CHUNK = 512
+N_CHUNKS = COLS // CHUNK
+EPS = 1e-12
+
+FLOPS = 2 * B * L * E * COLS
+
+SWEEP = 2048
+SWEEPS = [(c, min(SWEEP, COLS - c)) for c in range(0, COLS, SWEEP)]
+GROUP_HEADS = 3
+GROUP_COLS = GROUP_HEADS * HEAD_COLS
+N_GROUPS = (H + GROUP_HEADS - 1) // GROUP_HEADS
+CODE_TILE_BYTES = 4 * 2 * SWEEP
+CODE_BUFS = 6
+PASS_SPLIT = [(4, 3), (4, 3), (4, 3), (4, 3), (2, 2, 2, 1), (4, 3)]
+SCALE_SPLIT = [((0, 4), (4, 7))] * 5 + [((0, 7),)]
+SCALE_QUEUE = "sync"
+
+
+def tile_selfattention_pa_kernel(tc, x_words, x_scales, W_words, W_scales, b, out_0, out_1, out_2):
+    nc = tc.nc
+    outs = (out_0, out_1, out_2)
+
+    with ExitStack() as ctx:
+        const = ctx.enter_context(tc.tile_pool(name="const", bufs=1))
+        codes = ctx.enter_context(tc.tile_pool(name="codes", bufs=CODE_BUFS))
+        ypool = ctx.enter_context(tc.tile_pool(name="ypool", bufs=3))
+        stats = ctx.enter_context(tc.tile_pool(name="stats", bufs=3))
+        psum = ctx.enter_context(tc.psum_pool(name="psum", bufs=8))
+        ctx.enter_context(tc.manual_schedule())
+
+        warm = const.tile([P, 2], F32, name="warm")
+        nc.vector.memset(warm[:], 0.0)
+        x_raw = const.tile([P, PASSES, 2 * P], U8, name="x_raw", align_bytes=64)
+        xs_raw = const.tile([P, PASSES, P], U8, name="xs_raw", align_bytes=64)
+        x_codes = const.tile([P, PASSES, 2 * P], U8, name="x_codes", align_bytes=64)
+        x_planes = const.tile([P, PASSES, P], U8, name="x_planes", align_bytes=64)
+        nc.vector.memset(xs_raw[:].bitcast(I32), 0)
+
+        brow = const.tile([P, CHUNK], BF16, name="brow")
+        nc.gpsimd.memset(brow[:], 0.0)
+        nc.scalar.dma_start(out=brow[0:N_CHUNKS, :], in_=b.rearrange("(j n) -> j n", n=CHUNK))
+        nc.scalar.activation(out=warm[:, 1:2], in_=warm[:, 0:1], func=ACT.Square)
+        minus_half = const.tile([P, 2 * GROUP_HEADS], F32, name="minus_half")
+        nc.gpsimd.memset(minus_half[:], -0.5)
+        ident = const.tile([P, P], BF16, name="ident")
+        make_identity(nc, ident[:])
+
+        planes = []
+        for s, (c0, ws) in enumerate(SWEEPS):
+            pl = const.tile([P, PASSES, ws], U8, name="planes%d" % s, align_bytes=64)
+            planes.append(pl)
+            if s < 2:
+                nc.vector.memset(pl[:].bitcast(I32), 0)
+            else:
+                nc.gpsimd.memset(pl[:].bitcast(F32), 0.0)
+
+        jobs = [("x",)]
+        tile_no = 0
+        for s in range(len(SWEEPS)):
+            sweep_jobs = []
+            g0 = 0
+            for ng in PASS_SPLIT[s]:
+                sweep_jobs.append(("codes", tile_no, s, g0, ng))
+                tile_no += 1
+                g0 += ng
+            if s == 0:
+                jobs.append(sweep_jobs[0])
+                jobs.append(("scales", 0))
+                jobs.extend(sweep_jobs[1:])
+            elif s == len(SWEEPS) - 2:
+                jobs.append(("scales", s))
+                jobs.append(("scales", s + 1))
+                jobs.extend(sweep_jobs)
+            elif s == len(SWEEPS) - 1:
+                jobs.extend(sweep_jobs)
+            else:
+                jobs.append(("scales", s))
+                jobs.extend(sweep_jobs)
+
+        cursor = [0]
+        code_views = {}
+
+        def load_x():
+            nc.sync.dma_start(out=x_raw[:].bitcast(I32), in_=x_words.rearrange("g p n -> p g n").bitcast(I32))
+            for r in range(4):
+                nc.sync.dma_start(
+                    out=xs_raw[r:P:32, :, :].bitcast(I32),
+                    in_=x_scales[:, r:16:4, :].rearrange("g q n -> q g n").bitcast(I32),
+                )
+
+        def load_scales(s):
+            c0, ws = SWEEPS[s]
+            for ga, gb in SCALE_SPLIT[s]:
+                for r in range(4):
+                    dst = planes[s][r:P:32, ga:gb, :]
+                    src = W_scales[ga:gb, r:16:4, c0 : c0 + ws].rearrange("g q n -> q g n")
+                    if SCALE_QUEUE == "sync":
+                        nc.sync.dma_start(out=dst.bitcast(I32), in_=src.bitcast(I32))
+                    else:
+                        nc.gpsimd.dma_start(out=dst.bitcast(F32), in_=src.bitcast(F32))
+
+        def load_codes(t, s, g0, ng):
+            c0, ws = SWEEPS[s]
+            cw = codes.tile([P, CODE_TILE_BYTES], U8, tag="cw", align_bytes=64)
+            view = cw[:, 0 : ng * 2 * ws].rearrange("p (g n) -> p g n", g=ng)
+            nc.sync.dma_start(
+                out=view.bitcast(I32),
+                in_=W_words[g0 : g0 + ng, :, 2 * c0 : 2 * (c0 + ws)].rearrange("g p n -> p g n").bitcast(I32),
+            )
+            for gi in range(ng):
+                code_views[(s, g0 + gi)] = (view, gi, t, gi == ng - 1)
+
+        def emit_loads(max_tile):
+            while cursor[0] < len(jobs):
+                job = jobs[cursor[0]]
+                if job[0] == "codes" and job[1] > max_tile:
+                    break
+                if job[0] == "x":
+                    load_x()
+                elif job[0] == "scales":
+                    load_scales(job[1])
+                else:
+                    load_codes(job[1], job[2], job[3], job[4])
+                cursor[0] += 1
+
+        emit_loads(CODE_BUFS - 1)
+
+        for bb in range(B):
+            nc.vector.tensor_copy(
+                out=x_codes[:].rearrange("p g (l b e) -> p g l b e", b=B, e=2)[:, :, :, bb, :],
+                in_=x_raw[:].rearrange("p g (b l e) -> p g b l e", b=B, e=2)[:, :, bb, :, :],
+            )
+        nc.vector.tensor_copy(
+            out=x_planes[:].rearrange("p g (l b) -> p g b l", b=B),
+            in_=xs_raw[:].rearrange("p g (b l) -> p g b l", b=B),
+        )
+
+        bias = []
+        for j in range(N_CHUNKS):
+            pb = psum.tile([P, CHUNK], F32, tag="acc")
+            nc.tensor.matmul(out=pb[:], lhsT=ident[:, j : j + 1].to_broadcast([P, P]), rhs=brow[:], start=True, stop=True)
+            bj = const.tile([P, CHUNK], BF16, name="bias%d" % j)
+            bias.append(bj)
+            if j % 3 == 2:
+                nc.vector.tensor_copy(out=bj[:], in_=pb[:])
+            else:
+                nc.scalar.copy(out=bj[:], in_=pb[:])
+
+        junk = const.tile([P, HD], F32, name="junk")
+        ytile = {}
+
+        def y_of(grp):
+            if grp not in ytile:
+                yt = ypool.tile([P, GROUP_COLS], F32, tag="y")
+                ytile[grp] = yt
+            return ytile[grp]
+
+        def multiply(s):
+            c0, ws = SWEEPS[s]
+            accs = []
+            for j in range(ws // CHUNK):
+                acc = psum.tile([P, CHUNK], F32, tag="acc")
+                accs.append(acc)
+            for g in range(PASSES):
+                view, gi, t, last = code_views[(s, g)]
+                for j in range(ws // CHUNK):
+                    nc.tensor.matmul_mx(
+                        out=accs[j][:],
+                        lhsT=x_codes[:, g, :].bitcast(FP4X4),
+                        lhsT_scale=x_planes[:, g, :],
+                        rhs=view[:, gi, 2 * CHUNK * j : 2 * CHUNK * (j + 1)].bitcast(FP4X4),
+                        rhs_scale=planes[s][:, g, CHUNK * j : CHUNK * (j + 1)],
+                        start=(g == 0),
+                        stop=(g == PASSES - 1),
+                    )
+                if last:
+                    emit_loads(t + CODE_BUFS)
+            return accs
+
+        def add_bias(s, accs):
+            c0, ws = SWEEPS[s]
+            for j in range(ws // CHUNK):
+                lo = c0 + CHUNK * j
+                while lo < c0 + CHUNK * (j + 1):
+                    grp = min(lo // GROUP_COLS, N_GROUPS - 1)
+                    hi = min(c0 + CHUNK * (j + 1), (grp + 1) * GROUP_COLS)
+                    a = lo - c0 - CHUNK * j
+                    w = hi - lo
+                    off = lo - grp * GROUP_COLS
+                    nc.vector.tensor_tensor(
+                        out=y_of(grp)[:, off : off + w],
+                        in0=accs[j][:, a : a + w],
+                        in1=bias[(c0 // CHUNK) + j][:, a : a + w],
+                        op=ALU.add,
+                    )
+                    lo = hi
+
+        def finish_group(grp):
+            h0 = grp * GROUP_HEADS
+            nh = min(GROUP_HEADS, H - h0)
+            yv = ytile[grp][:, 0 : nh * HEAD_COLS].rearrange("p (h j c) -> p h j c", j=3, c=HD)
+
+            def store(j):
+                for bb in range(B):
+                    nc.scalar.dma_start(
+                        out=outs[j][bb, h0 : h0 + nh, :, :].rearrange("h l c -> l h c"),
+                        in_=yv[bb:P:2, :, j, :],
+                    )
+
+            store(2)
+            ss = stats.tile([P, 2 * GROUP_HEADS], F32, tag="ss")
+            rn = stats.tile([P, 2 * GROUP_HEADS], F32, tag="rn")
+            for h in range(nh):
+                for j in range(2):
+                    i = 2 * h + j
+                    nc.scalar.activation(out=junk[:], in_=yv[:, h, j, :], func=ACT.Square, accum_out=ss[:, i : i + 1])
+            nc.gpsimd.tensor_scalar_max(out=ss[:, 0 : 2 * nh], in0=ss[:, 0 : 2 * nh], scalar1=EPS * EPS)
+            nc.gpsimd.tensor_tensor(out=rn[:, 0 : 2 * nh], in0=ss[:, 0 : 2 * nh], in1=minus_half[:, 0 : 2 * nh], op=ALU.pow)
+            for h in range(nh):
+                for j in range(2):
+                    i = 2 * h + j
+                    nc.scalar.activation(out=yv[:, h, j, :], in_=yv[:, h, j, :], func=ACT.Copy, scale=rn[:, i : i + 1])
+            store(0)
+            store(1)
+
+        for s in range(len(SWEEPS)):
+            accs = multiply(s)
+            add_bias(s, accs)
+            finish_group(s)

@@ -24,15 +24,19 @@ EPS = 1e-12
 FLOPS = 2 * B * L * E * COLS
 
 SWEEP = 2048
-SWEEPS = [(c, min(SWEEP, COLS - c)) for c in range(0, COLS, SWEEP)]
+SWEEP_WIDTHS = [2048, 2048, 2048, 2048, 1024, 1024, 512]
+SWEEPS = [(sum(SWEEP_WIDTHS[:i]), SWEEP_WIDTHS[i]) for i in range(len(SWEEP_WIDTHS))]
+GROUP_H0 = [0] + [(c + w) // HEAD_COLS for c, w in SWEEPS]
 GROUP_HEADS = 3
 GROUP_COLS = GROUP_HEADS * HEAD_COLS
-N_GROUPS = (H + GROUP_HEADS - 1) // GROUP_HEADS
+GROUP_OF_HEAD = [s for s in range(len(SWEEPS)) for h in range(GROUP_H0[s], GROUP_H0[s + 1])]
 CODE_TILE_BYTES = 4 * 2 * SWEEP
 CODE_BUFS = 6
-PASS_SPLIT = [(4, 3), (4, 3), (4, 3), (4, 3), (2, 2, 2, 1), (4, 3)]
-SCALE_SPLIT = [((0, 4), (4, 7))] * 5 + [((0, 7),)]
-SCALE_QUEUE = "sync"
+PASS_SPLIT = [(4, 3)] * 7
+BLOCKS = [(0, 2048), (2048, 2048), (4096, 2048), (6144, 2048), (8192, 2560)]
+BLOCK_OF_SWEEP = [0, 1, 2, 3, 4, 4, 4]
+SCALE_QUEUE = "gpsimd"
+SYNC_STORE_FROM = 3
 
 
 def tile_selfattention_pa_kernel(tc, x_words, x_scales, W_words, W_scales, b, out_0, out_1, out_2):
@@ -42,7 +46,7 @@ def tile_selfattention_pa_kernel(tc, x_words, x_scales, W_words, W_scales, b, ou
     with ExitStack() as ctx:
         const = ctx.enter_context(tc.tile_pool(name="const", bufs=1))
         codes = ctx.enter_context(tc.tile_pool(name="codes", bufs=CODE_BUFS))
-        ypool = ctx.enter_context(tc.tile_pool(name="ypool", bufs=3))
+        ypool = ctx.enter_context(tc.tile_pool(name="ypool", bufs=4))
         stats = ctx.enter_context(tc.tile_pool(name="stats", bufs=3))
         psum = ctx.enter_context(tc.psum_pool(name="psum", bufs=8))
         ctx.enter_context(tc.manual_schedule())
@@ -65,13 +69,11 @@ def tile_selfattention_pa_kernel(tc, x_words, x_scales, W_words, W_scales, b, ou
         make_identity(nc, ident[:])
 
         planes = []
-        for s, (c0, ws) in enumerate(SWEEPS):
+        for s, (c0, ws) in enumerate(BLOCKS):
             pl = const.tile([P, PASSES, ws], U8, name="planes%d" % s, align_bytes=64)
             planes.append(pl)
             if s < 2:
                 nc.vector.memset(pl[:].bitcast(I32), 0)
-            else:
-                nc.gpsimd.memset(pl[:].bitcast(F32), 0.0)
 
         jobs = [("x",)]
         tile_no = 0
@@ -82,19 +84,7 @@ def tile_selfattention_pa_kernel(tc, x_words, x_scales, W_words, W_scales, b, ou
                 sweep_jobs.append(("codes", tile_no, s, g0, ng))
                 tile_no += 1
                 g0 += ng
-            if s == 0:
-                jobs.append(sweep_jobs[0])
-                jobs.append(("scales", 0))
-                jobs.extend(sweep_jobs[1:])
-            elif s == len(SWEEPS) - 2:
-                jobs.append(("scales", s))
-                jobs.append(("scales", s + 1))
-                jobs.extend(sweep_jobs)
-            elif s == len(SWEEPS) - 1:
-                jobs.extend(sweep_jobs)
-            else:
-                jobs.append(("scales", s))
-                jobs.extend(sweep_jobs)
+            jobs.extend(sweep_jobs)
 
         cursor = [0]
         code_views = {}
@@ -108,8 +98,8 @@ def tile_selfattention_pa_kernel(tc, x_words, x_scales, W_words, W_scales, b, ou
                 )
 
         def load_scales(s):
-            c0, ws = SWEEPS[s]
-            for ga, gb in SCALE_SPLIT[s]:
+            c0, ws = BLOCKS[s]
+            for ga, gb in ((0, PASSES),):
                 for r in range(4):
                     dst = planes[s][r:P:32, ga:gb, :]
                     src = W_scales[ga:gb, r:16:4, c0 : c0 + ws].rearrange("g q n -> q g n")
@@ -143,6 +133,8 @@ def tile_selfattention_pa_kernel(tc, x_words, x_scales, W_words, W_scales, b, ou
                 cursor[0] += 1
 
         emit_loads(CODE_BUFS - 1)
+        load_scales(0)
+        load_scales(1)
 
         for bb in range(B):
             nc.vector.tensor_copy(
@@ -154,6 +146,9 @@ def tile_selfattention_pa_kernel(tc, x_words, x_scales, W_words, W_scales, b, ou
             in_=xs_raw[:].rearrange("p g (b l) -> p g b l", b=B),
         )
 
+        nc.vector.memset(planes[2][:].bitcast(I32), 0)
+        load_scales(2)
+
         bias = []
         for j in range(N_CHUNKS):
             pb = psum.tile([P, CHUNK], F32, tag="acc")
@@ -164,6 +159,8 @@ def tile_selfattention_pa_kernel(tc, x_words, x_scales, W_words, W_scales, b, ou
                 nc.vector.tensor_copy(out=bj[:], in_=pb[:])
             else:
                 nc.scalar.copy(out=bj[:], in_=pb[:])
+            if j in (8, 14):
+                nc.vector.memset(planes[3 + (j - 8) // 6][:].bitcast(I32), 0)
 
         junk = const.tile([P, HD], F32, name="junk")
         ytile = {}
@@ -176,6 +173,8 @@ def tile_selfattention_pa_kernel(tc, x_words, x_scales, W_words, W_scales, b, ou
 
         def multiply(s):
             c0, ws = SWEEPS[s]
+            blk = BLOCK_OF_SWEEP[s]
+            boff = c0 - BLOCKS[blk][0]
             accs = []
             for j in range(ws // CHUNK):
                 acc = psum.tile([P, CHUNK], F32, tag="acc")
@@ -188,7 +187,7 @@ def tile_selfattention_pa_kernel(tc, x_words, x_scales, W_words, W_scales, b, ou
                         lhsT=x_codes[:, g, :].bitcast(FP4X4),
                         lhsT_scale=x_planes[:, g, :],
                         rhs=view[:, gi, 2 * CHUNK * j : 2 * CHUNK * (j + 1)].bitcast(FP4X4),
-                        rhs_scale=planes[s][:, g, CHUNK * j : CHUNK * (j + 1)],
+                        rhs_scale=planes[blk][:, g, boff + CHUNK * j : boff + CHUNK * (j + 1)],
                         start=(g == 0),
                         stop=(g == PASSES - 1),
                     )
@@ -201,11 +200,11 @@ def tile_selfattention_pa_kernel(tc, x_words, x_scales, W_words, W_scales, b, ou
             for j in range(ws // CHUNK):
                 lo = c0 + CHUNK * j
                 while lo < c0 + CHUNK * (j + 1):
-                    grp = min(lo // GROUP_COLS, N_GROUPS - 1)
-                    hi = min(c0 + CHUNK * (j + 1), (grp + 1) * GROUP_COLS)
+                    grp = GROUP_OF_HEAD[lo // HEAD_COLS]
+                    hi = min(c0 + CHUNK * (j + 1), GROUP_H0[grp + 1] * HEAD_COLS)
                     a = lo - c0 - CHUNK * j
                     w = hi - lo
-                    off = lo - grp * GROUP_COLS
+                    off = lo - GROUP_H0[grp] * HEAD_COLS
                     nc.vector.tensor_tensor(
                         out=y_of(grp)[:, off : off + w],
                         in0=accs[j][:, a : a + w],
@@ -215,18 +214,18 @@ def tile_selfattention_pa_kernel(tc, x_words, x_scales, W_words, W_scales, b, ou
                     lo = hi
 
         def finish_group(grp):
-            h0 = grp * GROUP_HEADS
-            nh = min(GROUP_HEADS, H - h0)
+            h0 = GROUP_H0[grp]
+            nh = GROUP_H0[grp + 1] - h0
             yv = ytile[grp][:, 0 : nh * HEAD_COLS].rearrange("p (h j c) -> p h j c", j=3, c=HD)
 
             def store(j):
+                queue = nc.sync if grp >= SYNC_STORE_FROM else nc.scalar
                 for bb in range(B):
-                    nc.scalar.dma_start(
+                    queue.dma_start(
                         out=outs[j][bb, h0 : h0 + nh, :, :].rearrange("h l c -> l h c"),
                         in_=yv[bb:P:2, :, j, :],
                     )
 
-            store(2)
             ss = stats.tile([P, 2 * GROUP_HEADS], F32, tag="ss")
             rn = stats.tile([P, 2 * GROUP_HEADS], F32, tag="rn")
             for h in range(nh):
@@ -235,6 +234,11 @@ def tile_selfattention_pa_kernel(tc, x_words, x_scales, W_words, W_scales, b, ou
                     nc.scalar.activation(out=junk[:], in_=yv[:, h, j, :], func=ACT.Square, accum_out=ss[:, i : i + 1])
             nc.gpsimd.tensor_scalar_max(out=ss[:, 0 : 2 * nh], in0=ss[:, 0 : 2 * nh], scalar1=EPS * EPS)
             nc.gpsimd.tensor_tensor(out=rn[:, 0 : 2 * nh], in0=ss[:, 0 : 2 * nh], in1=minus_half[:, 0 : 2 * nh], op=ALU.pow)
+            if grp == 0:
+                load_scales(3)
+            if grp == 1:
+                load_scales(4)
+            store(2)
             for h in range(nh):
                 for j in range(2):
                     i = 2 * h + j

@@ -33,9 +33,9 @@ GROUP_OF_HEAD = [s for s in range(len(SWEEPS)) for h in range(GROUP_H0[s], GROUP
 CODE_TILE_BYTES = 4 * 2 * SWEEP
 CODE_BUFS = 6
 PASS_SPLIT = [(4, 3)] * 7
-BLOCKS = [(0, 2048), (2048, 2048), (4096, 2048), (6144, 2048), (8192, 2560)]
-BLOCK_OF_SWEEP = [0, 1, 2, 3, 4, 4, 4]
-SCALE_QUEUE = "gpsimd"
+BLOCKS = [(0, 512), (512, 1536), (2048, 4096), (6144, 3584), (9728, 512), (10240, 512)]
+BLOCK_OF_CHUNK = [i for i in range(len(BLOCKS)) for c in range(BLOCKS[i][1] // CHUNK)]
+SCALE_QUEUE = "sync"
 SYNC_STORE_FROM = 3
 
 
@@ -57,7 +57,6 @@ def tile_selfattention_pa_kernel(tc, x_words, x_scales, W_words, W_scales, b, ou
         xs_raw = const.tile([P, PASSES, P], U8, name="xs_raw", align_bytes=64)
         x_codes = const.tile([P, PASSES, 2 * P], U8, name="x_codes", align_bytes=64)
         x_planes = const.tile([P, PASSES, P], U8, name="x_planes", align_bytes=64)
-        nc.vector.memset(xs_raw[:].bitcast(I32), 0)
 
         brow = const.tile([P, CHUNK], BF16, name="brow")
         nc.gpsimd.memset(brow[:], 0.0)
@@ -72,10 +71,11 @@ def tile_selfattention_pa_kernel(tc, x_words, x_scales, W_words, W_scales, b, ou
         for s, (c0, ws) in enumerate(BLOCKS):
             pl = const.tile([P, PASSES, ws], U8, name="planes%d" % s, align_bytes=64)
             planes.append(pl)
-            if s < 2:
-                nc.vector.memset(pl[:].bitcast(I32), 0)
+            nc.vector.memset(pl[:].bitcast(I32), 0)
+            if s == 1:
+                nc.vector.memset(xs_raw[:].bitcast(I32), 0)
 
-        jobs = [("x",)]
+        jobs = [("scales", 0), ("scales", 1), ("scales", 2), ("x",)] + [("scales", i) for i in range(3, len(BLOCKS))]
         tile_no = 0
         for s in range(len(SWEEPS)):
             sweep_jobs = []
@@ -133,8 +133,6 @@ def tile_selfattention_pa_kernel(tc, x_words, x_scales, W_words, W_scales, b, ou
                 cursor[0] += 1
 
         emit_loads(CODE_BUFS - 1)
-        load_scales(0)
-        load_scales(1)
 
         for bb in range(B):
             nc.vector.tensor_copy(
@@ -146,9 +144,6 @@ def tile_selfattention_pa_kernel(tc, x_words, x_scales, W_words, W_scales, b, ou
             in_=xs_raw[:].rearrange("p g (b l) -> p g b l", b=B),
         )
 
-        nc.vector.memset(planes[2][:].bitcast(I32), 0)
-        load_scales(2)
-
         bias = []
         for j in range(N_CHUNKS):
             pb = psum.tile([P, CHUNK], F32, tag="acc")
@@ -159,8 +154,6 @@ def tile_selfattention_pa_kernel(tc, x_words, x_scales, W_words, W_scales, b, ou
                 nc.vector.tensor_copy(out=bj[:], in_=pb[:])
             else:
                 nc.scalar.copy(out=bj[:], in_=pb[:])
-            if j in (8, 14):
-                nc.vector.memset(planes[3 + (j - 8) // 6][:].bitcast(I32), 0)
 
         junk = const.tile([P, HD], F32, name="junk")
         ytile = {}
@@ -173,8 +166,6 @@ def tile_selfattention_pa_kernel(tc, x_words, x_scales, W_words, W_scales, b, ou
 
         def multiply(s):
             c0, ws = SWEEPS[s]
-            blk = BLOCK_OF_SWEEP[s]
-            boff = c0 - BLOCKS[blk][0]
             accs = []
             for j in range(ws // CHUNK):
                 acc = psum.tile([P, CHUNK], F32, tag="acc")
@@ -182,12 +173,14 @@ def tile_selfattention_pa_kernel(tc, x_words, x_scales, W_words, W_scales, b, ou
             for g in range(PASSES):
                 view, gi, t, last = code_views[(s, g)]
                 for j in range(ws // CHUNK):
+                    blk = BLOCK_OF_CHUNK[c0 // CHUNK + j]
+                    boff = c0 + CHUNK * j - BLOCKS[blk][0]
                     nc.tensor.matmul_mx(
                         out=accs[j][:],
                         lhsT=x_codes[:, g, :].bitcast(FP4X4),
                         lhsT_scale=x_planes[:, g, :],
                         rhs=view[:, gi, 2 * CHUNK * j : 2 * CHUNK * (j + 1)].bitcast(FP4X4),
-                        rhs_scale=planes[blk][:, g, boff + CHUNK * j : boff + CHUNK * (j + 1)],
+                        rhs_scale=planes[blk][:, g, boff : boff + CHUNK],
                         start=(g == 0),
                         stop=(g == PASSES - 1),
                     )
@@ -234,10 +227,6 @@ def tile_selfattention_pa_kernel(tc, x_words, x_scales, W_words, W_scales, b, ou
                     nc.scalar.activation(out=junk[:], in_=yv[:, h, j, :], func=ACT.Square, accum_out=ss[:, i : i + 1])
             nc.gpsimd.tensor_scalar_max(out=ss[:, 0 : 2 * nh], in0=ss[:, 0 : 2 * nh], scalar1=EPS * EPS)
             nc.gpsimd.tensor_tensor(out=rn[:, 0 : 2 * nh], in0=ss[:, 0 : 2 * nh], in1=minus_half[:, 0 : 2 * nh], op=ALU.pow)
-            if grp == 0:
-                load_scales(3)
-            if grp == 1:
-                load_scales(4)
             store(2)
             for h in range(nh):
                 for j in range(2):

@@ -32,8 +32,8 @@ GROUP_COLS = GROUP_HEADS * HEAD_COLS
 GROUP_OF_HEAD = [s for s in range(len(SWEEPS)) for h in range(GROUP_H0[s], GROUP_H0[s + 1])]
 CODE_TILE_BYTES = 4 * 2 * SWEEP
 CODE_BUFS = 6
-PASS_SPLIT = [(4, 3)] * 7
-BLOCKS = [(0, 512), (512, 1536), (2048, 4096), (6144, 3584), (9728, 512), (10240, 512)]
+PASS_SPLIT = [(4, 3)] * 6 + [(6, 1)]
+BLOCKS = [(0, 1024), (1024, 3072), (4096, 6144), (10240, 512)]
 BLOCK_OF_CHUNK = [i for i in range(len(BLOCKS)) for c in range(BLOCKS[i][1] // CHUNK)]
 SCALE_QUEUE = "sync"
 SYNC_STORE_FROM = 3
@@ -75,7 +75,7 @@ def tile_selfattention_pa_kernel(tc, x_words, x_scales, W_words, W_scales, b, ou
             if s == 1:
                 nc.vector.memset(xs_raw[:].bitcast(I32), 0)
 
-        jobs = [("scales", 0), ("scales", 1), ("scales", 2), ("x",)] + [("scales", i) for i in range(3, len(BLOCKS))]
+        jobs = [("scales", 0), ("scales", 1), ("x",), ("scales", 2), ("scales", 3)]
         tile_no = 0
         for s in range(len(SWEEPS)):
             sweep_jobs = []
@@ -99,14 +99,11 @@ def tile_selfattention_pa_kernel(tc, x_words, x_scales, W_words, W_scales, b, ou
 
         def load_scales(s):
             c0, ws = BLOCKS[s]
-            for ga, gb in ((0, PASSES),):
-                for r in range(4):
-                    dst = planes[s][r:P:32, ga:gb, :]
-                    src = W_scales[ga:gb, r:16:4, c0 : c0 + ws].rearrange("g q n -> q g n")
-                    if SCALE_QUEUE == "sync":
-                        nc.sync.dma_start(out=dst.bitcast(I32), in_=src.bitcast(I32))
-                    else:
-                        nc.gpsimd.dma_start(out=dst.bitcast(F32), in_=src.bitcast(F32))
+            for q in range(8):
+                p = 32 * (q // 4) + q % 4
+                dst = planes[s][p:P:64, :, :]
+                src = W_scales[:, q:16:8, c0 : c0 + ws].rearrange("g q n -> q g n")
+                nc.sync.dma_start(out=dst.bitcast(I32), in_=src.bitcast(I32))
 
         def load_codes(t, s, g0, ng):
             c0, ws = SWEEPS[s]
@@ -156,6 +153,7 @@ def tile_selfattention_pa_kernel(tc, x_words, x_scales, W_words, W_scales, b, ou
                 nc.scalar.copy(out=bj[:], in_=pb[:])
 
         junk = const.tile([P, HD], F32, name="junk")
+        junk_v = const.tile([P, HD], F32, name="junk_v")
         ytile = {}
 
         def y_of(grp):
@@ -209,6 +207,7 @@ def tile_selfattention_pa_kernel(tc, x_words, x_scales, W_words, W_scales, b, ou
         def finish_group(grp):
             h0 = GROUP_H0[grp]
             nh = GROUP_H0[grp + 1] - h0
+            last_group = grp == len(SWEEPS) - 1
             yv = ytile[grp][:, 0 : nh * HEAD_COLS].rearrange("p (h j c) -> p h j c", j=3, c=HD)
 
             def store(j):
@@ -224,14 +223,23 @@ def tile_selfattention_pa_kernel(tc, x_words, x_scales, W_words, W_scales, b, ou
             for h in range(nh):
                 for j in range(2):
                     i = 2 * h + j
-                    nc.scalar.activation(out=junk[:], in_=yv[:, h, j, :], func=ACT.Square, accum_out=ss[:, i : i + 1])
+                    if last_group and j == 1:
+                        nc.vector.scalar_tensor_tensor(
+                            out=junk_v[:], in0=yv[:, h, j, :], scalar=1.0, in1=yv[:, h, j, :],
+                            op0=ALU.mult, op1=ALU.mult, accum_out=ss[:, i : i + 1],
+                        )
+                    else:
+                        nc.scalar.activation(out=junk[:], in_=yv[:, h, j, :], func=ACT.Square, accum_out=ss[:, i : i + 1])
             nc.gpsimd.tensor_scalar_max(out=ss[:, 0 : 2 * nh], in0=ss[:, 0 : 2 * nh], scalar1=EPS * EPS)
             nc.gpsimd.tensor_tensor(out=rn[:, 0 : 2 * nh], in0=ss[:, 0 : 2 * nh], in1=minus_half[:, 0 : 2 * nh], op=ALU.pow)
             store(2)
             for h in range(nh):
                 for j in range(2):
                     i = 2 * h + j
-                    nc.scalar.activation(out=yv[:, h, j, :], in_=yv[:, h, j, :], func=ACT.Copy, scale=rn[:, i : i + 1])
+                    if last_group and j == 1:
+                        nc.vector.tensor_scalar_mul(out=yv[:, h, j, :], in0=yv[:, h, j, :], scalar1=rn[:, i : i + 1])
+                    else:
+                        nc.scalar.activation(out=yv[:, h, j, :], in_=yv[:, h, j, :], func=ACT.Copy, scale=rn[:, i : i + 1])
             store(0)
             store(1)
 

@@ -37,6 +37,7 @@ BLOCKS = [(0, 1024), (1024, 3072), (4096, 6144), (10240, 512)]
 BLOCK_OF_CHUNK = [i for i in range(len(BLOCKS)) for c in range(BLOCKS[i][1] // CHUNK)]
 SCALE_QUEUE = "sync"
 SYNC_STORE_FROM = 3
+VECTOR_GROUPS = (4, 6)
 
 
 def tile_selfattention_pa_kernel(tc, x_words, x_scales, W_words, W_scales, b, out_0, out_1, out_2):
@@ -75,7 +76,7 @@ def tile_selfattention_pa_kernel(tc, x_words, x_scales, W_words, W_scales, b, ou
             if s == 1:
                 nc.vector.memset(xs_raw[:].bitcast(I32), 0)
 
-        jobs = [("scales", 0), ("scales", 1), ("x",), ("scales", 2), ("scales", 3)]
+        jobs = [("x",), ("scales", 0), ("scales", 1), ("xs",), ("scales", 2), ("scales", 3)]
         tile_no = 0
         for s in range(len(SWEEPS)):
             sweep_jobs = []
@@ -91,6 +92,8 @@ def tile_selfattention_pa_kernel(tc, x_words, x_scales, W_words, W_scales, b, ou
 
         def load_x():
             nc.sync.dma_start(out=x_raw[:].bitcast(I32), in_=x_words.rearrange("g p n -> p g n").bitcast(I32))
+
+        def load_xs():
             for r in range(4):
                 nc.sync.dma_start(
                     out=xs_raw[r:P:32, :, :].bitcast(I32),
@@ -123,6 +126,8 @@ def tile_selfattention_pa_kernel(tc, x_words, x_scales, W_words, W_scales, b, ou
                     break
                 if job[0] == "x":
                     load_x()
+                elif job[0] == "xs":
+                    load_xs()
                 elif job[0] == "scales":
                     load_scales(job[1])
                 else:
@@ -207,7 +212,7 @@ def tile_selfattention_pa_kernel(tc, x_words, x_scales, W_words, W_scales, b, ou
         def finish_group(grp):
             h0 = GROUP_H0[grp]
             nh = GROUP_H0[grp + 1] - h0
-            last_group = grp == len(SWEEPS) - 1
+            on_vector = grp in VECTOR_GROUPS
             yv = ytile[grp][:, 0 : nh * HEAD_COLS].rearrange("p (h j c) -> p h j c", j=3, c=HD)
 
             def store(j):
@@ -223,7 +228,7 @@ def tile_selfattention_pa_kernel(tc, x_words, x_scales, W_words, W_scales, b, ou
             for h in range(nh):
                 for j in range(2):
                     i = 2 * h + j
-                    if last_group and j == 1:
+                    if on_vector:
                         nc.vector.scalar_tensor_tensor(
                             out=junk_v[:], in0=yv[:, h, j, :], scalar=1.0, in1=yv[:, h, j, :],
                             op0=ALU.mult, op1=ALU.mult, accum_out=ss[:, i : i + 1],
@@ -236,7 +241,7 @@ def tile_selfattention_pa_kernel(tc, x_words, x_scales, W_words, W_scales, b, ou
             for h in range(nh):
                 for j in range(2):
                     i = 2 * h + j
-                    if last_group and j == 1:
+                    if on_vector:
                         nc.vector.tensor_scalar_mul(out=yv[:, h, j, :], in0=yv[:, h, j, :], scalar1=rn[:, i : i + 1])
                     else:
                         nc.scalar.activation(out=yv[:, h, j, :], in_=yv[:, h, j, :], func=ACT.Copy, scale=rn[:, i : i + 1])

from contextlib import ExitStack

import concourse.mybir as mybir
from concourse.masks import make_identity

F32 = mybir.dt.float32
BF16 = mybir.dt.bfloat16
U8 = mybir.dt.uint8
I32 = mybir.dt.int32
FP4X4 = mybir.dt.float4_e2m1fn_x4
ALU = mybir.AluOpType
ACT = mybir.ActivationFunctionType

P = 128
B, L, E, H = 2, 64, 3584, 16
HD = E // H
HEAD_COLS = 3 * HD
COLS = 3 * E
PASSES = E // 512
CHUNK = 512
N_CHUNKS = COLS // CHUNK
EPS = 1e-12

FLOPS = 2 * B * L * E * COLS

SWEEP = 2048
SWEEP_WIDTHS = [2048, 2048, 2048, 2048, 1024, 1024, 512]
SWEEPS = [(sum(SWEEP_WIDTHS[:i]), SWEEP_WIDTHS[i]) for i in range(len(SWEEP_WIDTHS))]
GROUP_H0 = [0] + [(c + w) // HEAD_COLS for c, w in SWEEPS]
GROUP_HEADS = 3
GROUP_COLS = GROUP_HEADS * HEAD_COLS
GROUP_OF_HEAD = [s for s in range(len(SWEEPS)) for h in range(GROUP_H0[s], GROUP_H0[s + 1])]
CODE_TILE_BYTES = 4 * 2 * SWEEP
CODE_BUFS = 6
PASS_SPLIT = [(4, 3)] * 6 + [(6, 1)]
BLOCKS = [(0, 1024), (1024, 3072), (4096, 6144), (10240, 512)]
BLOCK_OF_CHUNK = [i for i in range(len(BLOCKS)) for c in range(BLOCKS[i][1] // CHUNK)]
SCALE_QUEUE = "sync"
SYNC_STORE_FROM = 3
VECTOR_GROUPS = (4, 6)


def tile_selfattention_pa_kernel(tc, x_words, x_scales, W_words, W_scales, b, out_0, out_1, out_2):
    nc = tc.nc
    outs = (out_0, out_1, out_2)

    with ExitStack() as ctx:
        const = ctx.enter_context(tc.tile_pool(name="const", bufs=1))
        codes = ctx.enter_context(tc.tile_pool(name="codes", bufs=CODE_BUFS))
        ypool = ctx.enter_context(tc.tile_pool(name="ypool", bufs=4))
        stats = ctx.enter_context(tc.tile_pool(name="stats", bufs=3))
        psum = ctx.enter_context(tc.psum_pool(name="psum", bufs=8))
        ctx.enter_context(tc.manual_schedule())

        warm = const.tile([P, 2], F32, name="warm")
        nc.vector.memset(warm[:], 0.0)
        x_raw = const.tile([P, PASSES, 2 * P], U8, name="x_raw", align_bytes=64)
        xs_raw = const.tile([P, PASSES, P], U8, name="xs_raw", align_bytes=64)
        x_codes = const.tile([P, PASSES, 2 * P], U8, name="x_codes", align_bytes=64)
        x_planes = const.tile([P, PASSES, P], U8, name="x_planes", align_bytes=64)

        brow = const.tile([P, CHUNK], BF16, name="brow")
        nc.gpsimd.memset(brow[:], 0.0)
        nc.scalar.dma_start(out=brow[0:N_CHUNKS, :], in_=b.rearrange("(j n) -> j n", n=CHUNK))
        nc.scalar.activation(out=warm[:, 1:2], in_=warm[:, 0:1], func=ACT.Square)
        minus_half = const.tile([P, 2 * GROUP_HEADS], F32, name="minus_half")
        nc.gpsimd.memset(minus_half[:], -0.5)
        ident = const.tile([P, P], BF16, name="ident")
        make_identity(nc, ident[:])

        planes = []
        for s, (c0, ws) in enumerate(BLOCKS):
            pl = const.tile([P, PASSES, ws], U8, name="planes%d" % s, align_bytes=64)
            planes.append(pl)
            nc.vector.memset(pl[:].bitcast(I32), 0)
            if s == 1:
                nc.vector.memset(xs_raw[:].bitcast(I32), 0)

        jobs = [("x",), ("scales", 0), ("scales", 1), ("xs",), ("scales", 2), ("scales", 3)]
        tile_no = 0
        for s in range(len(SWEEPS)):
            sweep_jobs = []
            g0 = 0
            for ng in PASS_SPLIT[s]:
                sweep_jobs.append(("codes", tile_no, s, g0, ng))
                tile_no += 1
                g0 += ng
            jobs.extend(sweep_jobs)

        cursor = [0]
        code_views = {}

        def load_x():
            nc.sync.dma_start(out=x_raw[:].bitcast(I32), in_=x_words.rearrange("g p n -> p g n").bitcast(I32))

        def load_xs():
            for r in range(4):
                nc.sync.dma_start(
                    out=xs_raw[r:P:32, :, :].bitcast(I32),
                    in_=x_scales[:, r:16:4, :].rearrange("g q n -> q g n").bitcast(I32),
                )

        def load_scales(s):
            c0, ws = BLOCKS[s]
            for q in range(8):
                p = 32 * (q // 4) + q % 4
                dst = planes[s][p:P:64, :, :]
                src = W_scales[:, q:16:8, c0 : c0 + ws].rearrange("g q n -> q g n")
                nc.sync.dma_start(out=dst.bitcast(I32), in_=src.bitcast(I32))

        def load_codes(t, s, g0, ng):
            c0, ws = SWEEPS[s]
            cw = codes.tile([P, CODE_TILE_BYTES], U8, tag="cw", align_bytes=64)
            view = cw[:, 0 : ng * 2 * ws].rearrange("p (g n) -> p g n", g=ng)
            nc.sync.dma_start(
                out=view.bitcast(I32),
                in_=W_words[g0 : g0 + ng, :, 2 * c0 : 2 * (c0 + ws)].rearrange("g p n -> p g n").bitcast(I32),
            )
            for gi in range(ng):
                code_views[(s, g0 + gi)] = (view, gi, t, gi == ng - 1)

        def emit_loads(max_tile):
            while cursor[0] < len(jobs):
                job = jobs[cursor[0]]
                if job[0] == "codes" and job[1] > max_tile:
                    break
                if job[0] == "x":
                    load_x()
                elif job[0] == "xs":
                    load_xs()
                elif job[0] == "scales":
                    load_scales(job[1])
                else:
                    load_codes(job[1], job[2], job[3], job[4])
                cursor[0] += 1

        emit_loads(CODE_BUFS - 1)

        for bb in range(B):
            nc.vector.tensor_copy(
                out=x_codes[:].rearrange("p g (l b e) -> p g l b e", b=B, e=2)[:, :, :, bb, :],
                in_=x_raw[:].rearrange("p g (b l e) -> p g b l e", b=B, e=2)[:, :, bb, :, :],
            )
        nc.vector.tensor_copy(
            out=x_planes[:].rearrange("p g (l b) -> p g b l", b=B),
            in_=xs_raw[:].rearrange("p g (b l) -> p g b l", b=B),
        )

        bias = []
        for j in range(N_CHUNKS):
            pb = psum.tile([P, CHUNK], F32, tag="acc")
            nc.tensor.matmul(out=pb[:], lhsT=ident[:, j : j + 1].to_broadcast([P, P]), rhs=brow[:], start=True, stop=True)
            bj = const.tile([P, CHUNK], BF16, name="bias%d" % j)
            bias.append(bj)
            if j % 3 == 2:
                nc.vector.tensor_copy(out=bj[:], in_=pb[:])
            else:
                nc.scalar.copy(out=bj[:], in_=pb[:])

        junk = const.tile([P, HD], F32, name="junk")
        junk_v = const.tile([P, HD], F32, name="junk_v")
        ytile = {}

        def y_of(grp):
            if grp not in ytile:
                yt = ypool.tile([P, GROUP_COLS], F32, tag="y")
                ytile[grp] = yt
            return ytile[grp]

        def multiply(s):
            c0, ws = SWEEPS[s]
            accs = []
            for j in range(ws // CHUNK):
                acc = psum.tile([P, CHUNK], F32, tag="acc")
                accs.append(acc)
            for g in range(PASSES):
                view, gi, t, last = code_views[(s, g)]
                for j in range(ws // CHUNK):
                    blk = BLOCK_OF_CHUNK[c0 // CHUNK + j]
                    boff = c0 + CHUNK * j - BLOCKS[blk][0]
                    nc.tensor.matmul_mx(
                        out=accs[j][:],
                        lhsT=x_codes[:, g, :].bitcast(FP4X4),
                        lhsT_scale=x_planes[:, g, :],
                        rhs=view[:, gi, 2 * CHUNK * j : 2 * CHUNK * (j + 1)].bitcast(FP4X4),
                        rhs_scale=planes[blk][:, g, boff : boff + CHUNK],
                        start=(g == 0),
                        stop=(g == PASSES - 1),
                    )
                if last:
                    emit_loads(t + CODE_BUFS)
            return accs

        def add_bias(s, accs):
            c0, ws = SWEEPS[s]
            for j in range(ws // CHUNK):
                lo = c0 + CHUNK * j
                while lo < c0 + CHUNK * (j + 1):
                    grp = GROUP_OF_HEAD[lo // HEAD_COLS]
                    hi = min(c0 + CHUNK * (j + 1), GROUP_H0[grp + 1] * HEAD_COLS)
                    a = lo - c0 - CHUNK * j
                    w = hi - lo
                    off = lo - GROUP_H0[grp] * HEAD_COLS
                    nc.vector.tensor_tensor(
                        out=y_of(grp)[:, off : off + w],
                        in0=accs[j][:, a : a + w],
                        in1=bias[(c0 // CHUNK) + j][:, a : a + w],
                        op=ALU.add,
                    )
                    lo = hi

        def finish_group(grp):
            h0 = GROUP_H0[grp]
            nh = GROUP_H0[grp + 1] - h0
            on_vector = grp in VECTOR_GROUPS
            yv = ytile[grp][:, 0 : nh * HEAD_COLS].rearrange("p (h j c) -> p h j c", j=3, c=HD)

            def store(j):
                queue = nc.sync if grp >= SYNC_STORE_FROM else nc.scalar
                for bb in range(B):
                    queue.dma_start(
                        out=outs[j][bb, h0 : h0 + nh, :, :].rearrange("h l c -> l h c"),
                        in_=yv[bb:P:2, :, j, :],
                    )

            ss = stats.tile([P, 2 * GROUP_HEADS], F32, tag="ss")
            rn = stats.tile([P, 2 * GROUP_HEADS], F32, tag="rn")
            for h in range(nh):
                for j in range(2):
                    i = 2 * h + j
                    if on_vector:
                        nc.vector.scalar_tensor_tensor(
                            out=junk_v[:], in0=yv[:, h, j, :], scalar=1.0, in1=yv[:, h, j, :],
                            op0=ALU.mult, op1=ALU.mult, accum_out=ss[:, i : i + 1],
                        )
                    else:
                        nc.scalar.activation(out=junk[:], in_=yv[:, h, j, :], func=ACT.Square, accum_out=ss[:, i : i + 1])
            nc.gpsimd.tensor_scalar_max(out=ss[:, 0 : 2 * nh], in0=ss[:, 0 : 2 * nh], scalar1=EPS * EPS)
            nc.gpsimd.tensor_tensor(out=rn[:, 0 : 2 * nh], in0=ss[:, 0 : 2 * nh], in1=minus_half[:, 0 : 2 * nh], op=ALU.pow)
            store(2)
            for h in range(nh):
                for j in range(2):
                    i = 2 * h + j
                    if on_vector:
                        nc.vector.tensor_scalar_mul(out=yv[:, h, j, :], in0=yv[:, h, j, :], scalar1=rn[:, i : i + 1])
                    else:
                        nc.scalar.activation(out=yv[:, h, j, :], in_=yv[:, h, j, :], func=ACT.Copy, scale=rn[:, i : i + 1])
            store(0)
            store(1)

        for s in range(len(SWEEPS)):
            accs = multiply(s)
            add_bias(s, accs)
            finish_group(s)
